import numpy as np
import ml_dtypes


def mxq(x, axis, fmt="e4m3"):
    dtype, down = {"e4m3": (ml_dtypes.float8_e4m3fn, 7), "e5m2": (ml_dtypes.float8_e5m2, 14)}[fmt]
    v = np.moveaxis(np.asarray(x, np.float32).astype(ml_dtypes.bfloat16).astype(np.float64), axis, -1)
    blocks = v.reshape(v.shape[:-1] + (-1, 32))
    amax = np.abs(blocks).max(-1, keepdims=True)
    byte = np.maximum(np.where(amax > 0, np.frexp(amax)[1] - 1 + 127, 0) - down, 1)
    scale = np.exp2(byte - 127.0)
    codes = (blocks / scale).astype(np.float32).astype(dtype).astype(np.float64)
    return np.moveaxis((codes * scale).reshape(v.shape), -1, axis)


WIDE = False


def mx_kscale(k):
    if not WIDE:
        return np.ones(k)
    levels = np.array([10, -10, 5, -5, 0])
    a = np.random.permutation(np.resize(levels, k // 512 * 4)).reshape(k // 512, 4)
    idx = np.arange(k)
    return np.exp2(a[idx // 512, idx % 128 // 32])


BF16 = ml_dtypes.bfloat16


def bf(x):
    return np.asarray(x, np.float32).astype(BF16)


def f64(x):
    return np.asarray(x).astype(np.float64)


B, DH, DO, L = 128, 256, 1024, 128


def setup_inputs():
    s = mx_kscale(2 * DH)
    t = mx_kscale(DO)
    return {"sbj_vec": bf(np.random.standard_normal((B, DH)) * s[:DH]),
            "obj_vec": bf(np.random.standard_normal((B, DH)) * s[DH:]),
            "W1": bf(np.random.standard_normal((2 * DH, DO)) * 1.28 / np.sqrt(2 * DH) / s[:, None] * t),
            "b1": bf(np.random.standard_normal(DO) * 0.1 * t),
            "W2": bf(np.random.standard_normal((DO, DO)) * 12.0 / DO / t[:, None]),
            "b2": bf(np.random.standard_normal(DO) * 0.1),
            "label_vecs": bf(np.random.standard_normal((L, DO)) * 8.0 / np.sqrt(DO))}


def reference(sbj_vec, obj_vec, W1, b1, W2, b2, label_vecs):
    x = np.concatenate([f64(sbj_vec), f64(obj_vec)], axis=1)
    hidden = (mxq(np.maximum(x, 0.0), 1, "e4m3") @ mxq(f64(W1), 0, "e4m3")) + f64(b1)
    emb = (mxq(np.maximum(hidden, 0.0), 1, "e4m3") @ mxq(f64(W2), 0, "e4m3")) + f64(b2)
    lab = f64(label_vecs)
    scores = np.empty((emb.shape[0], lab.shape[0]))
    for l in range(lab.shape[0]):
        diff = np.maximum(lab[l][None, :] - emb, 0.0)
        scores[:, l] = -np.sqrt(np.sum(diff * diff, axis=1))
    return scores

@@ -1,0 +1,203 @@
+from contextlib import ExitStack
+
+import concourse.mybir as mybir
+from concourse.masks import make_identity
+
+BF16 = mybir.dt.bfloat16
+F32 = mybir.dt.float32
+U32 = mybir.dt.uint32
+U8 = mybir.dt.uint8
+FP8X4 = mybir.dt.float8_e4m3fn_x4
+ALU = mybir.AluOpType
+ACT = mybir.ActivationFunctionType
+
+P = 128
+PACK = 4
+K_PASS = P * PACK
+B, DH, DO, L = 128, 256, 1024, 128
+K1 = 2 * DH
+PASSES2 = DO // K_PASS
+CHUNKS = DO // P
+BANK = 512
+CHUNKS_PER_BANK = BANK // P
+HALVES = CHUNKS // CHUNKS_PER_BANK
+PIECE = 256
+
+FLOPS = 2 * B * K1 * DO + 2 * B * DO * DO + 4 * B * L * DO
+
+
+def quantise_weight_piece(nc, stage, index, rows, codes, scales):
+    grouped = stage.tile([P, PIECE, PACK], BF16, align_bytes=64)
+    dst = grouped[:].rearrange("p (c i) t -> p c t i", i=4)
+    src = rows.rearrange("p t (c i) -> p c t i", i=4)
+    if index % 3 == 2:
+        nc.scalar.copy(out=dst, in_=src)
+    else:
+        nc.vector.tensor_copy(out=dst, in_=src)
+    nc.vector.quantize_mx(
+        out=codes.bitcast(FP8X4),
+        scales=scales,
+        in_=grouped[:].rearrange("p n t -> p (n t)"),
+    )
+
+
+def tile_relationembedding_s_kernel(tc, sbj_vec, obj_vec, W1, b1, W2, b2, label_vecs, out):
+    nc = tc.nc
+    with ExitStack() as ctx:
+        keep = ctx.enter_context(tc.tile_pool(name="keep", bufs=1))
+        stage = ctx.enter_context(tc.tile_pool(name="stage", bufs=4))
+        work = ctx.enter_context(tc.tile_pool(name="work", bufs=6))
+        setup_psum = ctx.enter_context(tc.psum_pool(name="setup_psum", bufs=2))
+        score_psum = ctx.enter_context(tc.psum_pool(name="score_psum", bufs=6))
+
+        x_sb = keep.tile([P, K1], BF16)
+        nc.sync.dma_start(out=x_sb[:, 0:DH], in_=sbj_vec)
+        nc.sync.dma_start(out=x_sb[:, DH:K1], in_=obj_vec)
+        w1_raw = keep.tile([P, PACK, DO], BF16)
+        nc.sync.dma_start(out=w1_raw[:], in_=W1.rearrange("(t p) n -> p t n", p=P))
+        bias_rows = keep.tile([P, P], BF16)
+        nc.vector.memset(bias_rows[:], 0.0)
+        nc.sync.dma_start(out=bias_rows[0:CHUNKS, :], in_=b1.rearrange("(m p) -> m p", p=P))
+        nc.sync.dma_start(out=bias_rows[CHUNKS : 2 * CHUNKS, :], in_=b2.rearrange("(m p) -> m p", p=P))
+        w2_raw = keep.tile([P, PASSES2 * PACK, DO], BF16)
+        w2_view = W2.rearrange("(gt p) n -> p gt n", p=P)
+        label_sb = keep.tile([P, DO], BF16)
+        nc.sync.dma_start(out=w2_raw[:, :, 0:BANK], in_=w2_view[:, :, 0:BANK])
+        nc.sync.dma_start(out=label_sb[:], in_=label_vecs)
+        nc.sync.dma_start(out=w2_raw[:, :, BANK:DO], in_=w2_view[:, :, BANK:DO])
+
+        ident_bf = keep.tile([P, P], BF16)
+        make_identity(nc, ident_bf[:])
+        ident_f32 = keep.tile([P, P], F32)
+        make_identity(nc, ident_f32[:])
+        one = keep.tile([P, 1], F32)
+        nc.vector.memset(one[:], 1.0)
+        nc.scalar.sqrt(out=one[:], in_=one[:])
+
+        xt_ps = setup_psum.tile([P, PACK, B], BF16, tag="setup")
+        for t in range(PACK):
+            nc.tensor.transpose(xt_ps[:, t, :], x_sb[:, t * P : (t + 1) * P], ident_bf[:])
+        x_grouped = keep.tile([P, B, PACK], BF16, align_bytes=64)
+        nc.vector.tensor_scalar_max(out=x_grouped[:], in0=xt_ps[:].rearrange("p t b -> p b t"), scalar1=0.0)
+        x_codes = keep.tile([P, B], U32, align_bytes=64)
+        x_scales = keep.tile([P, B], U8, align_bytes=64)
+        nc.vector.quantize_mx(
+            out=x_codes[:].bitcast(FP8X4), scales=x_scales[:], in_=x_grouped[:].rearrange("p b t -> p (b t)")
+        )
+
+        bias_ps = setup_psum.tile([P, P], BF16, tag="setup")
+        nc.tensor.transpose(bias_ps[:], bias_rows[:], ident_bf[:])
+        bias_cols = keep.tile([P, 2 * CHUNKS], F32)
+        nc.vector.tensor_copy(out=bias_cols[:], in_=bias_ps[:, 0 : 2 * CHUNKS])
+
+        w1_codes = keep.tile([P, DO], U32, align_bytes=64)
+        w1_scales = keep.tile([P, DO], U8, align_bytes=64)
+        piece_index = 0
+        for n0 in range(0, DO, PIECE):
+            cols = slice(n0, n0 + PIECE)
+            quantise_weight_piece(nc, stage, piece_index, w1_raw[:, :, cols], w1_codes[:, cols], w1_scales[:, cols])
+            piece_index += 1
+
+        h_codes = keep.tile([P, PASSES2, B], U32, align_bytes=64)
+        h_scales = keep.tile([P, PASSES2, B], U8, align_bytes=64)
+        for g in range(PASSES2):
+            h_ps = setup_psum.tile([P, PACK, B], F32, tag="setup")
+            h_rows = stage.tile([P, PACK, B], BF16)
+            for t in range(PACK):
+                m = g * PACK + t
+                nc.tensor.matmul_mx(
+                    out=h_ps[:, t, :],
+                    lhsT=w1_codes[:, m * P : (m + 1) * P].bitcast(FP8X4),
+                    lhsT_scale=w1_scales[:, m * P : (m + 1) * P],
+                    rhs=x_codes[:].bitcast(FP8X4),
+                    rhs_scale=x_scales[:],
+                    start=True,
+                    stop=True,
+                )
+            for t in range(PACK):
+                m = g * PACK + t
+                nc.scalar.activation(
+                    out=h_rows[:, t, :], in_=h_ps[:, t, :], func=ACT.Relu, bias=bias_cols[:, m : m + 1], scale=1.0
+                )
+            h_grouped = stage.tile([P, B, PACK], BF16, align_bytes=64)
+            nc.vector.tensor_copy(out=h_grouped[:], in_=h_rows[:].rearrange("p t b -> p b t"))
+            nc.vector.quantize_mx(
+                out=h_codes[:, g, :].bitcast(FP8X4),
+                scales=h_scales[:, g, :],
+                in_=h_grouped[:].rearrange("p b t -> p (b t)"),
+            )
+
+        label_ps = setup_psum.tile([P, CHUNKS, L], BF16, tag="setup")
+        for c in range(CHUNKS):
+            nc.tensor.transpose(label_ps[:, c, :], label_sb[:, c * P : (c + 1) * P], ident_bf[:])
+        label_t = keep.tile([P, CHUNKS, L], F32)
+        nc.scalar.copy(out=label_t[:], in_=label_ps[:])
+
+        w2_codes = keep.tile([P, PASSES2, DO], U32, align_bytes=64)
+        w2_scales = keep.tile([P, PASSES2, DO], U8, align_bytes=64)
+        for n0 in range(0, DO, PIECE):
+            cols = slice(n0, n0 + PIECE)
+            for g in range(PASSES2):
+                quantise_weight_piece(
+                    nc,
+                    stage,
+                    piece_index,
+                    w2_raw[:, g * PACK : (g + 1) * PACK, cols],
+                    w2_codes[:, g, cols],
+                    w2_scales[:, g, cols],
+                )
+                piece_index += 1
+
+        emb_t = keep.tile([P, CHUNKS, B], F32)
+        for half in range(HALVES):
+            e_ps = setup_psum.tile([P, CHUNKS_PER_BANK, B], F32, tag="setup")
+            for q in range(CHUNKS_PER_BANK):
+                c = half * CHUNKS_PER_BANK + q
+                for g in range(PASSES2):
+                    nc.tensor.matmul_mx(
+                        out=e_ps[:, q, :],
+                        lhsT=w2_codes[:, g, c * P : (c + 1) * P].bitcast(FP8X4),
+                        lhsT_scale=w2_scales[:, g, c * P : (c + 1) * P],
+                        rhs=h_codes[:, g, :].bitcast(FP8X4),
+                        rhs_scale=h_scales[:, g, :],
+                        start=(g == 0),
+                        stop=(g == PASSES2 - 1),
+                    )
+            for q in range(CHUNKS_PER_BANK):
+                c = half * CHUNKS_PER_BANK + q
+                nc.scalar.activation(
+                    out=emb_t[:, c, :],
+                    in_=e_ps[:, q, :],
+                    func=ACT.Identity,
+                    bias=bias_cols[:, CHUNKS + c : CHUNKS + c + 1],
+                    scale=1.0,
+                )
+
+        square_sums = keep.tile([P, HALVES, L], F32)
+        for half in range(HALVES):
+            for l in range(L):
+                neg_relu = work.tile([P, BANK], F32)
+                flipped = score_psum.tile([P, BANK], F32)
+                for q in range(CHUNKS_PER_BANK):
+                    c = half * CHUNKS_PER_BANK + q
+                    cols = slice(q * P, (q + 1) * P)
+                    nc.vector.tensor_scalar(
+                        out=neg_relu[:, cols],
+                        in0=emb_t[:, c, :],
+                        scalar1=label_t[:, c, l : l + 1],
+                        scalar2=0.0,
+                        op0=ALU.subtract,
+                        op1=ALU.min,
+                    )
+                    nc.tensor.transpose(flipped[:, cols], neg_relu[:, cols], ident_f32[:])
+                squares = work.tile([P, BANK], F32)
+                nc.scalar.activation(
+                    out=squares[:], in_=flipped[:], func=ACT.Square, accum_out=square_sums[:, half, l : l + 1]
+                )
+
+        total = keep.tile([P, L], F32)
+        nc.vector.tensor_add(out=total[:], in0=square_sums[:, 0, :], in1=square_sums[:, 1, :])
+        nc.scalar.sqrt(out=total[:], in_=total[:])
+        scores = keep.tile([P, L], F32)
+        nc.vector.tensor_scalar_mul(out=scores[:], in0=total[:], scalar1=-1.0)
+        nc.sync.dma_start(out=out, in_=scores[:])

@@ -22,6 +22,9 @@ BANK = 512
 CHUNKS_PER_BANK = BANK // P
 HALVES = CHUNKS // CHUNKS_PER_BANK
 PIECE = 256
+N_VECTOR_WAY = 24
+N_SCALAR_WAY = L - N_VECTOR_WAY
+LABELS_PER_BROADCAST = 2
 
 FLOPS = 2 * B * K1 * DO + 2 * B * DO * DO + 4 * B * L * DO
 
@@ -47,6 +50,7 @@ def tile_relationembedding_s_kernel(tc, sbj_vec, obj_vec, W1, b1, W2, b2, label_
         keep = ctx.enter_context(tc.tile_pool(name="keep", bufs=1))
         stage = ctx.enter_context(tc.tile_pool(name="stage", bufs=4))
         work = ctx.enter_context(tc.tile_pool(name="work", bufs=6))
+        wide = ctx.enter_context(tc.tile_pool(name="wide", bufs=2))
         setup_psum = ctx.enter_context(tc.psum_pool(name="setup_psum", bufs=2))
         score_psum = ctx.enter_context(tc.psum_pool(name="score_psum", bufs=6))
 
@@ -65,6 +69,13 @@ def tile_relationembedding_s_kernel(tc, sbj_vec, obj_vec, W1, b1, W2, b2, label_
         nc.sync.dma_start(out=w2_raw[:, :, 0:BANK], in_=w2_view[:, :, 0:BANK])
         nc.sync.dma_start(out=label_sb[:], in_=label_vecs)
         nc.sync.dma_start(out=w2_raw[:, :, BANK:DO], in_=w2_view[:, :, BANK:DO])
+        label_bcast = keep.tile([P, N_VECTOR_WAY, DO], BF16)
+        for i0 in range(0, N_VECTOR_WAY, LABELS_PER_BROADCAST):
+            rows = label_vecs[N_SCALAR_WAY + i0 : N_SCALAR_WAY + i0 + LABELS_PER_BROADCAST, :]
+            nc.sync.dma_start(
+                out=label_bcast[:, i0 : i0 + LABELS_PER_BROADCAST, :].rearrange("p l d -> p (l d)"),
+                in_=rows.rearrange("l d -> (l d)").partition_broadcast(P),
+            )
 
         ident_bf = keep.tile([P, P], BF16)
         make_identity(nc, ident_bf[:])
@@ -173,9 +184,19 @@ def tile_relationembedding_s_kernel(tc, sbj_vec, obj_vec, W1, b1, W2, b2, label_
                     scale=1.0,
                 )
 
-        square_sums = keep.tile([P, HALVES, L], F32)
+        emb_rows = keep.tile([P, DO], F32)
         for half in range(HALVES):
-            for l in range(L):
+            rows_ps = setup_psum.tile([P, BANK], F32, tag="setup")
+            for q in range(CHUNKS_PER_BANK):
+                c = half * CHUNKS_PER_BANK + q
+                nc.tensor.transpose(rows_ps[:, q * P : (q + 1) * P], emb_t[:, c, :], ident_f32[:])
+            nc.vector.tensor_copy(out=emb_rows[:, half * BANK : (half + 1) * BANK], in_=rows_ps[:])
+
+        square_sums = keep.tile([P, HALVES, N_SCALAR_WAY], F32)
+        total = keep.tile([P, L], F32)
+
+        def scalar_way(l):
+            for half in range(HALVES):
                 neg_relu = work.tile([P, BANK], F32)
                 flipped = score_psum.tile([P, BANK], F32)
                 for q in range(CHUNKS_PER_BANK):
@@ -195,8 +216,36 @@ def tile_relationembedding_s_kernel(tc, sbj_vec, obj_vec, W1, b1, W2, b2, label_
                     out=squares[:], in_=flipped[:], func=ACT.Square, accum_out=square_sums[:, half, l : l + 1]
                 )
 
-        total = keep.tile([P, L], F32)
-        nc.vector.tensor_add(out=total[:], in0=square_sums[:, 0, :], in1=square_sums[:, 1, :])
+        def vector_way_difference(i):
+            diff = wide.tile([P, DO], F32)
+            nc.vector.tensor_sub(out=diff[:], in0=label_bcast[:, i, :], in1=emb_rows[:])
+            return diff
+
+        def vector_way_sum(i, diff):
+            products = wide.tile([P, DO], F32)
+            nc.vector.scalar_tensor_tensor(
+                out=products[:],
+                in0=diff[:],
+                scalar=0.0,
+                in1=diff[:],
+                op0=ALU.max,
+                op1=ALU.mult,
+                accum_out=total[:, N_SCALAR_WAY + i : N_SCALAR_WAY + i + 1],
+            )
+
+        steps = 2 * N_VECTOR_WAY
+        steps_done = 0
+        diff = None
+        for l in range(N_SCALAR_WAY):
+            scalar_way(l)
+            while steps_done * N_SCALAR_WAY < (l + 1) * steps:
+                if steps_done % 2 == 0:
+                    diff = vector_way_difference(steps_done // 2)
+                else:
+                    vector_way_sum(steps_done // 2, diff)
+                steps_done += 1
+
+        nc.vector.tensor_add(out=total[:, 0:N_SCALAR_WAY], in0=square_sums[:, 0, :], in1=square_sums[:, 1, :])
         nc.scalar.sqrt(out=total[:], in_=total[:])
         scores = keep.tile([P, L], F32)
         nc.vector.tensor_scalar_mul(out=scores[:], in0=total[:], scalar1=-1.0)

@@ -22,7 +22,7 @@ BANK = 512
 CHUNKS_PER_BANK = BANK // P
 HALVES = CHUNKS // CHUNKS_PER_BANK
 PIECE = 256
-N_VECTOR_WAY = 24
+N_VECTOR_WAY = 20
 N_SCALAR_WAY = L - N_VECTOR_WAY
 LABELS_PER_BROADCAST = 2
 

@@ -22,7 +22,7 @@ BANK = 512
 CHUNKS_PER_BANK = BANK // P
 HALVES = CHUNKS // CHUNKS_PER_BANK
 PIECE = 256
-N_VECTOR_WAY = 20
+N_VECTOR_WAY = 24
 N_SCALAR_WAY = L - N_VECTOR_WAY
 LABELS_PER_BROADCAST = 2
 
@@ -236,14 +236,15 @@ def tile_relationembedding_s_kernel(tc, sbj_vec, obj_vec, W1, b1, W2, b2, label_
         steps = 2 * N_VECTOR_WAY
         steps_done = 0
         diff = None
-        for l in range(N_SCALAR_WAY):
-            scalar_way(l)
-            while steps_done * N_SCALAR_WAY < (l + 1) * steps:
-                if steps_done % 2 == 0:
-                    diff = vector_way_difference(steps_done // 2)
-                else:
-                    vector_way_sum(steps_done // 2, diff)
-                steps_done += 1
+        with tc.manual_schedule():
+            for l in range(N_SCALAR_WAY):
+                scalar_way(l)
+                while steps_done * N_SCALAR_WAY < (l + 1) * steps:
+                    if steps_done % 2 == 0:
+                        diff = vector_way_difference(steps_done // 2)
+                    else:
+                        vector_way_sum(steps_done // 2, diff)
+                    steps_done += 1
 
         nc.vector.tensor_add(out=total[:, 0:N_SCALAR_WAY], in0=square_sums[:, 0, :], in1=square_sums[:, 1, :])
         nc.scalar.sqrt(out=total[:], in_=total[:])

@@ -21,60 +21,65 @@ CHUNKS = DO // P
 BANK = 512
 CHUNKS_PER_BANK = BANK // P
 HALVES = CHUNKS // CHUNKS_PER_BANK
-PIECE = 256
-N_VECTOR_WAY = 24
+RUN = 4
+N_VECTOR_WAY = 22
 N_SCALAR_WAY = L - N_VECTOR_WAY
 LABELS_PER_BROADCAST = 2
 
 FLOPS = 2 * B * K1 * DO + 2 * B * DO * DO + 4 * B * L * DO
 
 
-def quantise_weight_piece(nc, stage, index, rows, codes, scales):
-    grouped = stage.tile([P, PIECE, PACK], BF16, align_bytes=64)
-    dst = grouped[:].rearrange("p (c i) t -> p c t i", i=4)
-    src = rows.rearrange("p t (c i) -> p c t i", i=4)
-    if index % 3 == 2:
-        nc.scalar.copy(out=dst, in_=src)
-    else:
-        nc.vector.tensor_copy(out=dst, in_=src)
-    nc.vector.quantize_mx(
-        out=codes.bitcast(FP8X4),
-        scales=scales,
-        in_=grouped[:].rearrange("p n t -> p (n t)"),
-    )
+def regroup_weights(nc, stage, raw):
+    grouped = stage.tile([P, BANK, PACK], BF16, align_bytes=64)
+    dst = grouped[:].rearrange("p (c i) t -> p c t i", i=RUN)
+    src = raw.rearrange("p t (c i) -> p c t i", i=RUN)
+    runs = BANK // RUN
+    nc.vector.tensor_copy(out=dst[:, 0 : runs // 2], in_=src[:, 0 : runs // 2])
+    nc.scalar.copy(out=dst[:, runs // 2 : runs], in_=src[:, runs // 2 : runs])
+    return grouped
+
+
+def quantise(nc, grouped, codes, scales):
+    nc.vector.quantize_mx(out=codes.bitcast(FP8X4), scales=scales, in_=grouped.rearrange("p n t -> p (n t)"))
 
 
 def tile_relationembedding_s_kernel(tc, sbj_vec, obj_vec, W1, b1, W2, b2, label_vecs, out):
     nc = tc.nc
     with ExitStack() as ctx:
+        ctx.enter_context(tc.manual_schedule())
         keep = ctx.enter_context(tc.tile_pool(name="keep", bufs=1))
-        stage = ctx.enter_context(tc.tile_pool(name="stage", bufs=4))
+        stage = ctx.enter_context(tc.tile_pool(name="stage", bufs=3))
         work = ctx.enter_context(tc.tile_pool(name="work", bufs=6))
         wide = ctx.enter_context(tc.tile_pool(name="wide", bufs=2))
-        setup_psum = ctx.enter_context(tc.psum_pool(name="setup_psum", bufs=2))
-        score_psum = ctx.enter_context(tc.psum_pool(name="score_psum", bufs=6))
+        setup_psum = ctx.enter_context(tc.psum_pool(name="setup_psum", bufs=3))
+        score_psum = ctx.enter_context(tc.psum_pool(name="score_psum", bufs=5))
 
         x_sb = keep.tile([P, K1], BF16)
         nc.sync.dma_start(out=x_sb[:, 0:DH], in_=sbj_vec)
         nc.sync.dma_start(out=x_sb[:, DH:K1], in_=obj_vec)
-        w1_raw = keep.tile([P, PACK, DO], BF16)
-        nc.sync.dma_start(out=w1_raw[:], in_=W1.rearrange("(t p) n -> p t n", p=P))
         bias_rows = keep.tile([P, P], BF16)
         nc.vector.memset(bias_rows[:], 0.0)
         nc.sync.dma_start(out=bias_rows[0:CHUNKS, :], in_=b1.rearrange("(m p) -> m p", p=P))
         nc.sync.dma_start(out=bias_rows[CHUNKS : 2 * CHUNKS, :], in_=b2.rearrange("(m p) -> m p", p=P))
-        w2_raw = keep.tile([P, PASSES2 * PACK, DO], BF16)
-        w2_view = W2.rearrange("(gt p) n -> p gt n", p=P)
+        w1_raw = keep.tile([P, PACK, DO], BF16)
+        w1_view = W1.rearrange("(t p) n -> p t n", p=P)
+        for half in range(HALVES):
+            cols = slice(half * BANK, (half + 1) * BANK)
+            nc.sync.dma_start(out=w1_raw[:, :, cols], in_=w1_view[:, :, cols])
+        w2_raw = keep.tile([P, PASSES2, PACK, DO], BF16)
+        w2_view = W2.rearrange("(g t p) n -> p g t n", t=PACK, p=P)
         label_sb = keep.tile([P, DO], BF16)
-        nc.sync.dma_start(out=w2_raw[:, :, 0:BANK], in_=w2_view[:, :, 0:BANK])
+        for half in range(HALVES):
+            cols = slice(half * BANK, (half + 1) * BANK)
+            for g in range(PASSES2):
+                nc.sync.dma_start(out=w2_raw[:, g, :, cols], in_=w2_view[:, g, :, cols])
         nc.sync.dma_start(out=label_sb[:], in_=label_vecs)
-        nc.sync.dma_start(out=w2_raw[:, :, BANK:DO], in_=w2_view[:, :, BANK:DO])
         label_bcast = keep.tile([P, N_VECTOR_WAY, DO], BF16)
         for i0 in range(0, N_VECTOR_WAY, LABELS_PER_BROADCAST):
-            rows = label_vecs[N_SCALAR_WAY + i0 : N_SCALAR_WAY + i0 + LABELS_PER_BROADCAST, :]
+            own_rows = label_vecs[N_SCALAR_WAY + i0 : N_SCALAR_WAY + i0 + LABELS_PER_BROADCAST, :]
             nc.sync.dma_start(
                 out=label_bcast[:, i0 : i0 + LABELS_PER_BROADCAST, :].rearrange("p l d -> p (l d)"),
-                in_=rows.rearrange("l d -> (l d)").partition_broadcast(P),
+                in_=own_rows.rearrange("l d -> (l d)").partition_broadcast(P),
             )
 
         ident_bf = keep.tile([P, P], BF16)
@@ -90,34 +95,30 @@ def tile_relationembedding_s_kernel(tc, sbj_vec, obj_vec, W1, b1, W2, b2, label_
             nc.tensor.transpose(xt_ps[:, t, :], x_sb[:, t * P : (t + 1) * P], ident_bf[:])
         x_grouped = keep.tile([P, B, PACK], BF16, align_bytes=64)
         nc.vector.tensor_scalar_max(out=x_grouped[:], in0=xt_ps[:].rearrange("p t b -> p b t"), scalar1=0.0)
-        x_codes = keep.tile([P, B], U32, align_bytes=64)
-        x_scales = keep.tile([P, B], U8, align_bytes=64)
-        nc.vector.quantize_mx(
-            out=x_codes[:].bitcast(FP8X4), scales=x_scales[:], in_=x_grouped[:].rearrange("p b t -> p (b t)")
-        )
 
         bias_ps = setup_psum.tile([P, P], BF16, tag="setup")
         nc.tensor.transpose(bias_ps[:], bias_rows[:], ident_bf[:])
         bias_cols = keep.tile([P, 2 * CHUNKS], F32)
         nc.vector.tensor_copy(out=bias_cols[:], in_=bias_ps[:, 0 : 2 * CHUNKS])
 
+        x_codes = keep.tile([P, B], U32, align_bytes=64)
+        x_scales = keep.tile([P, B], U8, align_bytes=64)
+        quantise(nc, x_grouped[:], x_codes[:], x_scales[:])
+
         w1_codes = keep.tile([P, DO], U32, align_bytes=64)
         w1_scales = keep.tile([P, DO], U8, align_bytes=64)
-        piece_index = 0
-        for n0 in range(0, DO, PIECE):
-            cols = slice(n0, n0 + PIECE)
-            quantise_weight_piece(nc, stage, piece_index, w1_raw[:, :, cols], w1_codes[:, cols], w1_scales[:, cols])
-            piece_index += 1
-
-        h_codes = keep.tile([P, PASSES2, B], U32, align_bytes=64)
-        h_scales = keep.tile([P, PASSES2, B], U8, align_bytes=64)
-        for g in range(PASSES2):
-            h_ps = setup_psum.tile([P, PACK, B], F32, tag="setup")
-            h_rows = stage.tile([P, PACK, B], BF16)
-            for t in range(PACK):
-                m = g * PACK + t
+        w1_grouped = []
+        for half in range(HALVES):
+            w1_grouped.append(regroup_weights(nc, stage, w1_raw[:, :, half * BANK : (half + 1) * BANK]))
+        h_banks = []
+        for half in range(HALVES):
+            cols = slice(half * BANK, (half + 1) * BANK)
+            quantise(nc, w1_grouped[half][:], w1_codes[:, cols], w1_scales[:, cols])
+            h_ps = setup_psum.tile([P, CHUNKS_PER_BANK, B], F32, tag="setup")
+            for q in range(CHUNKS_PER_BANK):
+                m = half * CHUNKS_PER_BANK + q
                 nc.tensor.matmul_mx(
-                    out=h_ps[:, t, :],
+                    out=h_ps[:, q, :],
                     lhsT=w1_codes[:, m * P : (m + 1) * P].bitcast(FP8X4),
                     lhsT_scale=w1_scales[:, m * P : (m + 1) * P],
                     rhs=x_codes[:].bitcast(FP8X4),
@@ -125,18 +126,49 @@ def tile_relationembedding_s_kernel(tc, sbj_vec, obj_vec, W1, b1, W2, b2, label_
                     start=True,
                     stop=True,
                 )
-            for t in range(PACK):
-                m = g * PACK + t
-                nc.scalar.activation(
-                    out=h_rows[:, t, :], in_=h_ps[:, t, :], func=ACT.Relu, bias=bias_cols[:, m : m + 1], scale=1.0
-                )
-            h_grouped = stage.tile([P, B, PACK], BF16, align_bytes=64)
-            nc.vector.tensor_copy(out=h_grouped[:], in_=h_rows[:].rearrange("p t b -> p b t"))
-            nc.vector.quantize_mx(
-                out=h_codes[:, g, :].bitcast(FP8X4),
-                scales=h_scales[:, g, :],
-                in_=h_grouped[:].rearrange("p b t -> p (b t)"),
+            h_banks.append(h_ps)
+
+        w2_codes = keep.tile([P, PASSES2, DO], U32, align_bytes=64)
+        w2_scales = keep.tile([P, PASSES2, DO], U8, align_bytes=64)
+        w2_pieces = [(half, g) for half in range(HALVES) for g in range(PASSES2)]
+
+        def regroup_w2_piece(piece):
+            half, g = piece
+            return regroup_weights(nc, stage, w2_raw[:, g, :, half * BANK : (half + 1) * BANK])
+
+        w2_grouped = [regroup_w2_piece(w2_pieces[0])]
+
+        h_rows = keep.tile([P, PASSES2, PACK, B], BF16)
+        for t in range(PACK):
+            nc.scalar.activation(
+                out=h_rows[:, 0, t, :], in_=h_banks[0][:, t, :], func=ACT.Relu, bias=bias_cols[:, t : t + 1], scale=1.0
             )
+        for t in range(PACK):
+            nc.vector.tensor_scalar(
+                out=h_rows[:, 1, t, :],
+                in0=h_banks[1][:, t, :],
+                scalar1=bias_cols[:, PACK + t : PACK + t + 1],
+                scalar2=0.0,
+                op0=ALU.add,
+                op1=ALU.max,
+            )
+        h_grouped = keep.tile([P, PASSES2, B, PACK], BF16, align_bytes=64)
+        nc.vector.tensor_copy(out=h_grouped[:], in_=h_rows[:].rearrange("p g t b -> p g b t"))
+        w2_grouped.append(regroup_w2_piece(w2_pieces[1]))
+        h_codes = keep.tile([P, PASSES2, B], U32, align_bytes=64)
+        h_scales = keep.tile([P, PASSES2, B], U8, align_bytes=64)
+        quantise(
+            nc,
+            h_grouped[:].rearrange("p g b t -> p (g b) t"),
+            h_codes[:].rearrange("p g b -> p (g b)"),
+            h_scales[:].rearrange("p g b -> p (g b)"),
+        )
+        for index in range(len(w2_pieces)):
+            half, g = w2_pieces[index]
+            cols = slice(half * BANK, (half + 1) * BANK)
+            quantise(nc, w2_grouped[index][:], w2_codes[:, g, cols], w2_scales[:, g, cols])
+            if index + 2 < len(w2_pieces):
+                w2_grouped.append(regroup_w2_piece(w2_pieces[index + 2]))
 
         label_ps = setup_psum.tile([P, CHUNKS, L], BF16, tag="setup")
         for c in range(CHUNKS):
@@ -144,22 +176,8 @@ def tile_relationembedding_s_kernel(tc, sbj_vec, obj_vec, W1, b1, W2, b2, label_
         label_t = keep.tile([P, CHUNKS, L], F32)
         nc.scalar.copy(out=label_t[:], in_=label_ps[:])
 
-        w2_codes = keep.tile([P, PASSES2, DO], U32, align_bytes=64)
-        w2_scales = keep.tile([P, PASSES2, DO], U8, align_bytes=64)
-        for n0 in range(0, DO, PIECE):
-            cols = slice(n0, n0 + PIECE)
-            for g in range(PASSES2):
-                quantise_weight_piece(
-                    nc,
-                    stage,
-                    piece_index,
-                    w2_raw[:, g * PACK : (g + 1) * PACK, cols],
-                    w2_codes[:, g, cols],
-                    w2_scales[:, g, cols],
-                )
-                piece_index += 1
-
         emb_t = keep.tile([P, CHUNKS, B], F32)
+        e_banks = []
         for half in range(HALVES):
             e_ps = setup_psum.tile([P, CHUNKS_PER_BANK, B], F32, tag="setup")
             for q in range(CHUNKS_PER_BANK):
@@ -174,23 +192,17 @@ def tile_relationembedding_s_kernel(tc, sbj_vec, obj_vec, W1, b1, W2, b2, label_
                         start=(g == 0),
                         stop=(g == PASSES2 - 1),
                     )
+            e_banks.append(e_ps)
+        for half in range(HALVES):
             for q in range(CHUNKS_PER_BANK):
                 c = half * CHUNKS_PER_BANK + q
                 nc.scalar.activation(
                     out=emb_t[:, c, :],
-                    in_=e_ps[:, q, :],
+                    in_=e_banks[half][:, q, :],
                     func=ACT.Identity,
                     bias=bias_cols[:, CHUNKS + c : CHUNKS + c + 1],
                     scale=1.0,
                 )
-
-        emb_rows = keep.tile([P, DO], F32)
-        for half in range(HALVES):
-            rows_ps = setup_psum.tile([P, BANK], F32, tag="setup")
-            for q in range(CHUNKS_PER_BANK):
-                c = half * CHUNKS_PER_BANK + q
-                nc.tensor.transpose(rows_ps[:, q * P : (q + 1) * P], emb_t[:, c, :], ident_f32[:])
-            nc.vector.tensor_copy(out=emb_rows[:, half * BANK : (half + 1) * BANK], in_=rows_ps[:])
 
         square_sums = keep.tile([P, HALVES, N_SCALAR_WAY], F32)
         total = keep.tile([P, L], F32)
@@ -216,35 +228,50 @@ def tile_relationembedding_s_kernel(tc, sbj_vec, obj_vec, W1, b1, W2, b2, label_
                     out=squares[:], in_=flipped[:], func=ACT.Square, accum_out=square_sums[:, half, l : l + 1]
                 )
 
-        def vector_way_difference(i):
+        emb_rows = keep.tile([P, DO], F32)
+        rows_banks = {}
+        diffs = {}
+
+        def flip_emb_back(half):
+            rows_ps = setup_psum.tile([P, BANK], F32, tag="setup")
+            for q in range(CHUNKS_PER_BANK):
+                c = half * CHUNKS_PER_BANK + q
+                nc.tensor.transpose(rows_ps[:, q * P : (q + 1) * P], emb_t[:, c, :], ident_f32[:])
+            rows_banks[half] = rows_ps
+
+        def keep_emb_rows(half):
+            nc.vector.tensor_copy(out=emb_rows[:, half * BANK : (half + 1) * BANK], in_=rows_banks[half][:])
+
+        def difference(i):
             diff = wide.tile([P, DO], F32)
             nc.vector.tensor_sub(out=diff[:], in0=label_bcast[:, i, :], in1=emb_rows[:])
-            return diff
+            diffs[i] = diff
 
-        def vector_way_sum(i, diff):
+        def sum_of_squares(i):
             products = wide.tile([P, DO], F32)
             nc.vector.scalar_tensor_tensor(
                 out=products[:],
-                in0=diff[:],
+                in0=diffs[i][:],
                 scalar=0.0,
-                in1=diff[:],
+                in1=diffs[i][:],
                 op0=ALU.max,
                 op1=ALU.mult,
                 accum_out=total[:, N_SCALAR_WAY + i : N_SCALAR_WAY + i + 1],
             )
 
-        steps = 2 * N_VECTOR_WAY
+        vector_steps = [(flip_emb_back, half) for half in range(HALVES)]
+        vector_steps.extend([(keep_emb_rows, half) for half in range(HALVES)])
+        for i in range(N_VECTOR_WAY):
+            vector_steps.append((difference, i))
+            vector_steps.append((sum_of_squares, i))
+
         steps_done = 0
-        diff = None
-        with tc.manual_schedule():
-            for l in range(N_SCALAR_WAY):
-                scalar_way(l)
-                while steps_done * N_SCALAR_WAY < (l + 1) * steps:
-                    if steps_done % 2 == 0:
-                        diff = vector_way_difference(steps_done // 2)
-                    else:
-                        vector_way_sum(steps_done // 2, diff)
-                    steps_done += 1
+        for l in range(N_SCALAR_WAY):
+            scalar_way(l)
+            while steps_done * N_SCALAR_WAY < (l + 1) * len(vector_steps):
+                step, argument = vector_steps[steps_done]
+                step(argument)
+                steps_done += 1
 
         nc.vector.tensor_add(out=total[:, 0:N_SCALAR_WAY], in0=square_sums[:, 0, :], in1=square_sums[:, 1, :])
         nc.scalar.sqrt(out=total[:], in_=total[:])

@@ -22,7 +22,7 @@ BANK = 512
 CHUNKS_PER_BANK = BANK // P
 HALVES = CHUNKS // CHUNKS_PER_BANK
 RUN = 4
-N_VECTOR_WAY = 22
+N_VECTOR_WAY = 26
 N_SCALAR_WAY = L - N_VECTOR_WAY
 LABELS_PER_BROADCAST = 2
 
@@ -177,8 +177,9 @@ def tile_relationembedding_s_kernel(tc, sbj_vec, obj_vec, W1, b1, W2, b2, label_
         nc.scalar.copy(out=label_t[:], in_=label_ps[:])
 
         emb_t = keep.tile([P, CHUNKS, B], F32)
-        e_banks = []
-        for half in range(HALVES):
+        e_banks = {}
+
+        def emb_passes(half):
             e_ps = setup_psum.tile([P, CHUNKS_PER_BANK, B], F32, tag="setup")
             for q in range(CHUNKS_PER_BANK):
                 c = half * CHUNKS_PER_BANK + q
@@ -192,8 +193,9 @@ def tile_relationembedding_s_kernel(tc, sbj_vec, obj_vec, W1, b1, W2, b2, label_
                         start=(g == 0),
                         stop=(g == PASSES2 - 1),
                     )
-            e_banks.append(e_ps)
-        for half in range(HALVES):
+            e_banks[half] = e_ps
+
+        def emb_bias(half):
             for q in range(CHUNKS_PER_BANK):
                 c = half * CHUNKS_PER_BANK + q
                 nc.scalar.activation(
@@ -204,29 +206,31 @@ def tile_relationembedding_s_kernel(tc, sbj_vec, obj_vec, W1, b1, W2, b2, label_
                     scale=1.0,
                 )
 
+        emb_passes(0)
+        emb_bias(0)
+
         square_sums = keep.tile([P, HALVES, N_SCALAR_WAY], F32)
         total = keep.tile([P, L], F32)
 
-        def scalar_way(l):
-            for half in range(HALVES):
-                neg_relu = work.tile([P, BANK], F32)
-                flipped = score_psum.tile([P, BANK], F32)
-                for q in range(CHUNKS_PER_BANK):
-                    c = half * CHUNKS_PER_BANK + q
-                    cols = slice(q * P, (q + 1) * P)
-                    nc.vector.tensor_scalar(
-                        out=neg_relu[:, cols],
-                        in0=emb_t[:, c, :],
-                        scalar1=label_t[:, c, l : l + 1],
-                        scalar2=0.0,
-                        op0=ALU.subtract,
-                        op1=ALU.min,
-                    )
-                    nc.tensor.transpose(flipped[:, cols], neg_relu[:, cols], ident_f32[:])
-                squares = work.tile([P, BANK], F32)
-                nc.scalar.activation(
-                    out=squares[:], in_=flipped[:], func=ACT.Square, accum_out=square_sums[:, half, l : l + 1]
+        def scalar_way(half, l):
+            neg_relu = work.tile([P, BANK], F32)
+            flipped = score_psum.tile([P, BANK], F32)
+            for q in range(CHUNKS_PER_BANK):
+                c = half * CHUNKS_PER_BANK + q
+                cols = slice(q * P, (q + 1) * P)
+                nc.vector.tensor_scalar(
+                    out=neg_relu[:, cols],
+                    in0=emb_t[:, c, :],
+                    scalar1=label_t[:, c, l : l + 1],
+                    scalar2=0.0,
+                    op0=ALU.subtract,
+                    op1=ALU.min,
                 )
+                nc.tensor.transpose(flipped[:, cols], neg_relu[:, cols], ident_f32[:])
+            squares = work.tile([P, BANK], F32)
+            nc.scalar.activation(
+                out=squares[:], in_=flipped[:], func=ACT.Square, accum_out=square_sums[:, half, l : l + 1]
+            )
 
         emb_rows = keep.tile([P, DO], F32)
         rows_banks = {}
@@ -259,19 +263,24 @@ def tile_relationembedding_s_kernel(tc, sbj_vec, obj_vec, W1, b1, W2, b2, label_
                 accum_out=total[:, N_SCALAR_WAY + i : N_SCALAR_WAY + i + 1],
             )
 
-        vector_steps = [(flip_emb_back, half) for half in range(HALVES)]
-        vector_steps.extend([(keep_emb_rows, half) for half in range(HALVES)])
+        steps = [(emb_passes, 1), (emb_bias, 1)]
+        steps.extend([(flip_emb_back, half) for half in range(HALVES)])
+        steps.extend([(keep_emb_rows, half) for half in range(HALVES)])
         for i in range(N_VECTOR_WAY):
-            vector_steps.append((difference, i))
-            vector_steps.append((sum_of_squares, i))
+            steps.append((difference, i))
+            steps.append((sum_of_squares, i))
 
+        units = HALVES * N_SCALAR_WAY
+        units_done = 0
         steps_done = 0
-        for l in range(N_SCALAR_WAY):
-            scalar_way(l)
-            while steps_done * N_SCALAR_WAY < (l + 1) * len(vector_steps):
-                step, argument = vector_steps[steps_done]
-                step(argument)
-                steps_done += 1
+        for half in range(HALVES):
+            for l in range(N_SCALAR_WAY):
+                scalar_way(half, l)
+                units_done += 1
+                while steps_done * units < units_done * len(steps):
+                    step, argument = steps[steps_done]
+                    step(argument)
+                    steps_done += 1
 
         nc.vector.tensor_add(out=total[:, 0:N_SCALAR_WAY], in0=square_sums[:, 0, :], in1=square_sums[:, 1, :])
         nc.scalar.sqrt(out=total[:], in_=total[:])

@@ -22,9 +22,10 @@ BANK = 512
 CHUNKS_PER_BANK = BANK // P
 HALVES = CHUNKS // CHUNKS_PER_BANK
 RUN = 4
-N_VECTOR_WAY = 26
-N_SCALAR_WAY = L - N_VECTOR_WAY
+SECOND_WAY_LABELS = 22
+FIRST_WAY_LABELS = L - SECOND_WAY_LABELS
 LABELS_PER_BROADCAST = 2
+SQRT_GUARD = 1e-30
 
 FLOPS = 2 * B * K1 * DO + 2 * B * DO * DO + 4 * B * L * DO
 
@@ -68,15 +69,15 @@ def tile_relationembedding_s_kernel(tc, sbj_vec, obj_vec, W1, b1, W2, b2, label_
             nc.sync.dma_start(out=w1_raw[:, :, cols], in_=w1_view[:, :, cols])
         w2_raw = keep.tile([P, PASSES2, PACK, DO], BF16)
         w2_view = W2.rearrange("(g t p) n -> p g t n", t=PACK, p=P)
-        label_sb = keep.tile([P, DO], BF16)
         for half in range(HALVES):
             cols = slice(half * BANK, (half + 1) * BANK)
             for g in range(PASSES2):
                 nc.sync.dma_start(out=w2_raw[:, g, :, cols], in_=w2_view[:, g, :, cols])
+        label_sb = keep.tile([P, DO], BF16)
         nc.sync.dma_start(out=label_sb[:], in_=label_vecs)
-        label_bcast = keep.tile([P, N_VECTOR_WAY, DO], BF16)
-        for i0 in range(0, N_VECTOR_WAY, LABELS_PER_BROADCAST):
-            own_rows = label_vecs[N_SCALAR_WAY + i0 : N_SCALAR_WAY + i0 + LABELS_PER_BROADCAST, :]
+        label_bcast = keep.tile([P, SECOND_WAY_LABELS, DO], BF16)
+        for i0 in range(0, SECOND_WAY_LABELS, LABELS_PER_BROADCAST):
+            own_rows = label_vecs[FIRST_WAY_LABELS + i0 : FIRST_WAY_LABELS + i0 + LABELS_PER_BROADCAST, :]
             nc.sync.dma_start(
                 out=label_bcast[:, i0 : i0 + LABELS_PER_BROADCAST, :].rearrange("p l d -> p (l d)"),
                 in_=own_rows.rearrange("l d -> (l d)").partition_broadcast(P),
@@ -177,9 +178,8 @@ def tile_relationembedding_s_kernel(tc, sbj_vec, obj_vec, W1, b1, W2, b2, label_
         nc.scalar.copy(out=label_t[:], in_=label_ps[:])
 
         emb_t = keep.tile([P, CHUNKS, B], F32)
-        e_banks = {}
-
-        def emb_passes(half):
+        e_banks = []
+        for half in range(HALVES):
             e_ps = setup_psum.tile([P, CHUNKS_PER_BANK, B], F32, tag="setup")
             for q in range(CHUNKS_PER_BANK):
                 c = half * CHUNKS_PER_BANK + q
@@ -193,9 +193,8 @@ def tile_relationembedding_s_kernel(tc, sbj_vec, obj_vec, W1, b1, W2, b2, label_
                         start=(g == 0),
                         stop=(g == PASSES2 - 1),
                     )
-            e_banks[half] = e_ps
-
-        def emb_bias(half):
+            e_banks.append(e_ps)
+        for half in range(HALVES):
             for q in range(CHUNKS_PER_BANK):
                 c = half * CHUNKS_PER_BANK + q
                 nc.scalar.activation(
@@ -206,31 +205,29 @@ def tile_relationembedding_s_kernel(tc, sbj_vec, obj_vec, W1, b1, W2, b2, label_
                     scale=1.0,
                 )
 
-        emb_passes(0)
-        emb_bias(0)
-
-        square_sums = keep.tile([P, HALVES, N_SCALAR_WAY], F32)
+        square_sums = keep.tile([P, HALVES, FIRST_WAY_LABELS], F32)
         total = keep.tile([P, L], F32)
 
-        def scalar_way(half, l):
-            neg_relu = work.tile([P, BANK], F32)
-            flipped = score_psum.tile([P, BANK], F32)
-            for q in range(CHUNKS_PER_BANK):
-                c = half * CHUNKS_PER_BANK + q
-                cols = slice(q * P, (q + 1) * P)
-                nc.vector.tensor_scalar(
-                    out=neg_relu[:, cols],
-                    in0=emb_t[:, c, :],
-                    scalar1=label_t[:, c, l : l + 1],
-                    scalar2=0.0,
-                    op0=ALU.subtract,
-                    op1=ALU.min,
+        def first_way(l):
+            for half in range(HALVES):
+                neg_relu = work.tile([P, BANK], F32)
+                flipped = score_psum.tile([P, BANK], F32)
+                for q in range(CHUNKS_PER_BANK):
+                    c = half * CHUNKS_PER_BANK + q
+                    cols = slice(q * P, (q + 1) * P)
+                    nc.vector.tensor_scalar(
+                        out=neg_relu[:, cols],
+                        in0=emb_t[:, c, :],
+                        scalar1=label_t[:, c, l : l + 1],
+                        scalar2=0.0,
+                        op0=ALU.subtract,
+                        op1=ALU.min,
+                    )
+                    nc.tensor.transpose(flipped[:, cols], neg_relu[:, cols], ident_f32[:])
+                squares = work.tile([P, BANK], F32)
+                nc.scalar.activation(
+                    out=squares[:], in_=flipped[:], func=ACT.Square, accum_out=square_sums[:, half, l : l + 1]
                 )
-                nc.tensor.transpose(flipped[:, cols], neg_relu[:, cols], ident_f32[:])
-            squares = work.tile([P, BANK], F32)
-            nc.scalar.activation(
-                out=squares[:], in_=flipped[:], func=ACT.Square, accum_out=square_sums[:, half, l : l + 1]
-            )
 
         emb_rows = keep.tile([P, DO], F32)
         rows_banks = {}
@@ -260,30 +257,25 @@ def tile_relationembedding_s_kernel(tc, sbj_vec, obj_vec, W1, b1, W2, b2, label_
                 in1=diffs[i][:],
                 op0=ALU.max,
                 op1=ALU.mult,
-                accum_out=total[:, N_SCALAR_WAY + i : N_SCALAR_WAY + i + 1],
+                accum_out=total[:, FIRST_WAY_LABELS + i : FIRST_WAY_LABELS + i + 1],
             )
 
-        steps = [(emb_passes, 1), (emb_bias, 1)]
-        steps.extend([(flip_emb_back, half) for half in range(HALVES)])
-        steps.extend([(keep_emb_rows, half) for half in range(HALVES)])
-        for i in range(N_VECTOR_WAY):
-            steps.append((difference, i))
-            steps.append((sum_of_squares, i))
+        second_way_steps = [(flip_emb_back, half) for half in range(HALVES)]
+        second_way_steps.extend([(keep_emb_rows, half) for half in range(HALVES)])
+        for i in range(SECOND_WAY_LABELS):
+            second_way_steps.append((difference, i))
+            second_way_steps.append((sum_of_squares, i))
 
-        units = HALVES * N_SCALAR_WAY
-        units_done = 0
         steps_done = 0
-        for half in range(HALVES):
-            for l in range(N_SCALAR_WAY):
-                scalar_way(half, l)
-                units_done += 1
-                while steps_done * units < units_done * len(steps):
-                    step, argument = steps[steps_done]
-                    step(argument)
-                    steps_done += 1
+        for l in range(FIRST_WAY_LABELS):
+            first_way(l)
+            while steps_done * FIRST_WAY_LABELS < (l + 1) * len(second_way_steps):
+                step, argument = second_way_steps[steps_done]
+                step(argument)
+                steps_done += 1
 
-        nc.vector.tensor_add(out=total[:, 0:N_SCALAR_WAY], in0=square_sums[:, 0, :], in1=square_sums[:, 1, :])
-        nc.scalar.sqrt(out=total[:], in_=total[:])
+        nc.vector.tensor_add(out=total[:, 0:FIRST_WAY_LABELS], in0=square_sums[:, 0, :], in1=square_sums[:, 1, :])
+        nc.scalar.activation(out=total[:], in_=total[:], func=ACT.Sqrt, bias=SQRT_GUARD, scale=1.0)
         scores = keep.tile([P, L], F32)
         nc.vector.tensor_scalar_mul(out=scores[:], in0=total[:], scalar1=-1.0)
         nc.sync.dma_start(out=out, in_=scores[:])

from contextlib import ExitStack

import concourse.mybir as mybir
from concourse.masks import make_identity

BF16 = mybir.dt.bfloat16
F32 = mybir.dt.float32
U32 = mybir.dt.uint32
U8 = mybir.dt.uint8
FP8X4 = mybir.dt.float8_e4m3fn_x4
ALU = mybir.AluOpType
ACT = mybir.ActivationFunctionType

P = 128
PACK = 4
K_PASS = P * PACK
B, DH, DO, L = 128, 256, 1024, 128
K1 = 2 * DH
PASSES2 = DO // K_PASS
CHUNKS = DO // P
BANK = 512
CHUNKS_PER_BANK = BANK // P
HALVES = CHUNKS // CHUNKS_PER_BANK
RUN = 4
SECOND_WAY_LABELS = 22
FIRST_WAY_LABELS = L - SECOND_WAY_LABELS
LABELS_PER_BROADCAST = 2
SQRT_GUARD = 1e-30

FLOPS = 2 * B * K1 * DO + 2 * B * DO * DO + 4 * B * L * DO


def regroup_weights(nc, stage, raw):
    grouped = stage.tile([P, BANK, PACK], BF16, align_bytes=64)
    dst = grouped[:].rearrange("p (c i) t -> p c t i", i=RUN)
    src = raw.rearrange("p t (c i) -> p c t i", i=RUN)
    runs = BANK // RUN
    nc.vector.tensor_copy(out=dst[:, 0 : runs // 2], in_=src[:, 0 : runs // 2])
    nc.scalar.copy(out=dst[:, runs // 2 : runs], in_=src[:, runs // 2 : runs])
    return grouped


def quantise(nc, grouped, codes, scales):
    nc.vector.quantize_mx(out=codes.bitcast(FP8X4), scales=scales, in_=grouped.rearrange("p n t -> p (n t)"))


def tile_relationembedding_s_kernel(tc, sbj_vec, obj_vec, W1, b1, W2, b2, label_vecs, out):
    nc = tc.nc
    with ExitStack() as ctx:
        ctx.enter_context(tc.manual_schedule())
        keep = ctx.enter_context(tc.tile_pool(name="keep", bufs=1))
        stage = ctx.enter_context(tc.tile_pool(name="stage", bufs=3))
        work = ctx.enter_context(tc.tile_pool(name="work", bufs=6))
        wide = ctx.enter_context(tc.tile_pool(name="wide", bufs=2))
        setup_psum = ctx.enter_context(tc.psum_pool(name="setup_psum", bufs=3))
        score_psum = ctx.enter_context(tc.psum_pool(name="score_psum", bufs=5))

        x_sb = keep.tile([P, K1], BF16)
        nc.sync.dma_start(out=x_sb[:, 0:DH], in_=sbj_vec)
        nc.sync.dma_start(out=x_sb[:, DH:K1], in_=obj_vec)
        bias_rows = keep.tile([P, P], BF16)
        nc.vector.memset(bias_rows[:], 0.0)
        nc.sync.dma_start(out=bias_rows[0:CHUNKS, :], in_=b1.rearrange("(m p) -> m p", p=P))
        nc.sync.dma_start(out=bias_rows[CHUNKS : 2 * CHUNKS, :], in_=b2.rearrange("(m p) -> m p", p=P))
        w1_raw = keep.tile([P, PACK, DO], BF16)
        w1_view = W1.rearrange("(t p) n -> p t n", p=P)
        for half in range(HALVES):
            cols = slice(half * BANK, (half + 1) * BANK)
            nc.sync.dma_start(out=w1_raw[:, :, cols], in_=w1_view[:, :, cols])
        w2_raw = keep.tile([P, PASSES2, PACK, DO], BF16)
        w2_view = W2.rearrange("(g t p) n -> p g t n", t=PACK, p=P)
        for half in range(HALVES):
            cols = slice(half * BANK, (half + 1) * BANK)
            for g in range(PASSES2):
                nc.sync.dma_start(out=w2_raw[:, g, :, cols], in_=w2_view[:, g, :, cols])
        label_sb = keep.tile([P, DO], BF16)
        nc.sync.dma_start(out=label_sb[:], in_=label_vecs)
        label_bcast = keep.tile([P, SECOND_WAY_LABELS, DO], BF16)
        for i0 in range(0, SECOND_WAY_LABELS, LABELS_PER_BROADCAST):
            own_rows = label_vecs[FIRST_WAY_LABELS + i0 : FIRST_WAY_LABELS + i0 + LABELS_PER_BROADCAST, :]
            nc.sync.dma_start(
                out=label_bcast[:, i0 : i0 + LABELS_PER_BROADCAST, :].rearrange("p l d -> p (l d)"),
                in_=own_rows.rearrange("l d -> (l d)").partition_broadcast(P),
            )

        ident_bf = keep.tile([P, P], BF16)
        make_identity(nc, ident_bf[:])
        ident_f32 = keep.tile([P, P], F32)
        make_identity(nc, ident_f32[:])
        one = keep.tile([P, 1], F32)
        nc.vector.memset(one[:], 1.0)
        nc.scalar.sqrt(out=one[:], in_=one[:])

        xt_ps = setup_psum.tile([P, PACK, B], BF16, tag="setup")
        for t in range(PACK):
            nc.tensor.transpose(xt_ps[:, t, :], x_sb[:, t * P : (t + 1) * P], ident_bf[:])
        x_grouped = keep.tile([P, B, PACK], BF16, align_bytes=64)
        nc.vector.tensor_scalar_max(out=x_grouped[:], in0=xt_ps[:].rearrange("p t b -> p b t"), scalar1=0.0)

        bias_ps = setup_psum.tile([P, P], BF16, tag="setup")
        nc.tensor.transpose(bias_ps[:], bias_rows[:], ident_bf[:])
        bias_cols = keep.tile([P, 2 * CHUNKS], F32)
        nc.vector.tensor_copy(out=bias_cols[:], in_=bias_ps[:, 0 : 2 * CHUNKS])

        x_codes = keep.tile([P, B], U32, align_bytes=64)
        x_scales = keep.tile([P, B], U8, align_bytes=64)
        quantise(nc, x_grouped[:], x_codes[:], x_scales[:])

        w1_codes = keep.tile([P, DO], U32, align_bytes=64)
        w1_scales = keep.tile([P, DO], U8, align_bytes=64)
        w1_grouped = []
        for half in range(HALVES):
            w1_grouped.append(regroup_weights(nc, stage, w1_raw[:, :, half * BANK : (half + 1) * BANK]))
        h_banks = []
        for half in range(HALVES):
            cols = slice(half * BANK, (half + 1) * BANK)
            quantise(nc, w1_grouped[half][:], w1_codes[:, cols], w1_scales[:, cols])
            h_ps = setup_psum.tile([P, CHUNKS_PER_BANK, B], F32, tag="setup")
            for q in range(CHUNKS_PER_BANK):
                m = half * CHUNKS_PER_BANK + q
                nc.tensor.matmul_mx(
                    out=h_ps[:, q, :],
                    lhsT=w1_codes[:, m * P : (m + 1) * P].bitcast(FP8X4),
                    lhsT_scale=w1_scales[:, m * P : (m + 1) * P],
                    rhs=x_codes[:].bitcast(FP8X4),
                    rhs_scale=x_scales[:],
                    start=True,
                    stop=True,
                )
            h_banks.append(h_ps)

        w2_codes = keep.tile([P, PASSES2, DO], U32, align_bytes=64)
        w2_scales = keep.tile([P, PASSES2, DO], U8, align_bytes=64)
        w2_pieces = [(half, g) for half in range(HALVES) for g in range(PASSES2)]

        def regroup_w2_piece(piece):
            half, g = piece
            return regroup_weights(nc, stage, w2_raw[:, g, :, half * BANK : (half + 1) * BANK])

        w2_grouped = [regroup_w2_piece(w2_pieces[0])]

        h_rows = keep.tile([P, PASSES2, PACK, B], BF16)
        for t in range(PACK):
            nc.scalar.activation(
                out=h_rows[:, 0, t, :], in_=h_banks[0][:, t, :], func=ACT.Relu, bias=bias_cols[:, t : t + 1], scale=1.0
            )
        for t in range(PACK):
            nc.vector.tensor_scalar(
                out=h_rows[:, 1, t, :],
                in0=h_banks[1][:, t, :],
                scalar1=bias_cols[:, PACK + t : PACK + t + 1],
                scalar2=0.0,
                op0=ALU.add,
                op1=ALU.max,
            )
        h_grouped = keep.tile([P, PASSES2, B, PACK], BF16, align_bytes=64)
        nc.vector.tensor_copy(out=h_grouped[:], in_=h_rows[:].rearrange("p g t b -> p g b t"))
        w2_grouped.append(regroup_w2_piece(w2_pieces[1]))
        h_codes = keep.tile([P, PASSES2, B], U32, align_bytes=64)
        h_scales = keep.tile([P, PASSES2, B], U8, align_bytes=64)
        quantise(
            nc,
            h_grouped[:].rearrange("p g b t -> p (g b) t"),
            h_codes[:].rearrange("p g b -> p (g b)"),
            h_scales[:].rearrange("p g b -> p (g b)"),
        )
        for index in range(len(w2_pieces)):
            half, g = w2_pieces[index]
            cols = slice(half * BANK, (half + 1) * BANK)
            quantise(nc, w2_grouped[index][:], w2_codes[:, g, cols], w2_scales[:, g, cols])
            if index + 2 < len(w2_pieces):
                w2_grouped.append(regroup_w2_piece(w2_pieces[index + 2]))

        label_ps = setup_psum.tile([P, CHUNKS, L], BF16, tag="setup")
        for c in range(CHUNKS):
            nc.tensor.transpose(label_ps[:, c, :], label_sb[:, c * P : (c + 1) * P], ident_bf[:])
        label_t = keep.tile([P, CHUNKS, L], F32)
        nc.scalar.copy(out=label_t[:], in_=label_ps[:])

        emb_t = keep.tile([P, CHUNKS, B], F32)
        e_banks = []
        for half in range(HALVES):
            e_ps = setup_psum.tile([P, CHUNKS_PER_BANK, B], F32, tag="setup")
            for q in range(CHUNKS_PER_BANK):
                c = half * CHUNKS_PER_BANK + q
                for g in range(PASSES2):
                    nc.tensor.matmul_mx(
                        out=e_ps[:, q, :],
                        lhsT=w2_codes[:, g, c * P : (c + 1) * P].bitcast(FP8X4),
                        lhsT_scale=w2_scales[:, g, c * P : (c + 1) * P],
                        rhs=h_codes[:, g, :].bitcast(FP8X4),
                        rhs_scale=h_scales[:, g, :],
                        start=(g == 0),
                        stop=(g == PASSES2 - 1),
                    )
            e_banks.append(e_ps)
        for half in range(HALVES):
            for q in range(CHUNKS_PER_BANK):
                c = half * CHUNKS_PER_BANK + q
                nc.scalar.activation(
                    out=emb_t[:, c, :],
                    in_=e_banks[half][:, q, :],
                    func=ACT.Identity,
                    bias=bias_cols[:, CHUNKS + c : CHUNKS + c + 1],
                    scale=1.0,
                )

        square_sums = keep.tile([P, HALVES, FIRST_WAY_LABELS], F32)
        total = keep.tile([P, L], F32)

        def first_way(l):
            for half in range(HALVES):
                neg_relu = work.tile([P, BANK], F32)
                flipped = score_psum.tile([P, BANK], F32)
                for q in range(CHUNKS_PER_BANK):
                    c = half * CHUNKS_PER_BANK + q
                    cols = slice(q * P, (q + 1) * P)
                    nc.vector.tensor_scalar(
                        out=neg_relu[:, cols],
                        in0=emb_t[:, c, :],
                        scalar1=label_t[:, c, l : l + 1],
                        scalar2=0.0,
                        op0=ALU.subtract,
                        op1=ALU.min,
                    )
                    nc.tensor.transpose(flipped[:, cols], neg_relu[:, cols], ident_f32[:])
                squares = work.tile([P, BANK], F32)
                nc.scalar.activation(
                    out=squares[:], in_=flipped[:], func=ACT.Square, accum_out=square_sums[:, half, l : l + 1]
                )

        emb_rows = keep.tile([P, DO], F32)
        rows_banks = {}
        diffs = {}

        def flip_emb_back(half):
            rows_ps = setup_psum.tile([P, BANK], F32, tag="setup")
            for q in range(CHUNKS_PER_BANK):
                c = half * CHUNKS_PER_BANK + q
                nc.tensor.transpose(rows_ps[:, q * P : (q + 1) * P], emb_t[:, c, :], ident_f32[:])
            rows_banks[half] = rows_ps

        def keep_emb_rows(half):
            nc.vector.tensor_copy(out=emb_rows[:, half * BANK : (half + 1) * BANK], in_=rows_banks[half][:])

        def difference(i):
            diff = wide.tile([P, DO], F32)
            nc.vector.tensor_sub(out=diff[:], in0=label_bcast[:, i, :], in1=emb_rows[:])
            diffs[i] = diff

        def sum_of_squares(i):
            products = wide.tile([P, DO], F32)
            nc.vector.scalar_tensor_tensor(
                out=products[:],
                in0=diffs[i][:],
                scalar=0.0,
                in1=diffs[i][:],
                op0=ALU.max,
                op1=ALU.mult,
                accum_out=total[:, FIRST_WAY_LABELS + i : FIRST_WAY_LABELS + i + 1],
            )

        second_way_steps = [(flip_emb_back, half) for half in range(HALVES)]
        second_way_steps.extend([(keep_emb_rows, half) for half in range(HALVES)])
        for i in range(SECOND_WAY_LABELS):
            second_way_steps.append((difference, i))
            second_way_steps.append((sum_of_squares, i))

        steps_done = 0
        for l in range(FIRST_WAY_LABELS):
            first_way(l)
            while steps_done * FIRST_WAY_LABELS < (l + 1) * len(second_way_steps):
                step, argument = second_way_steps[steps_done]
                step(argument)
                steps_done += 1

        nc.vector.tensor_add(out=total[:, 0:FIRST_WAY_LABELS], in0=square_sums[:, 0, :], in1=square_sums[:, 1, :])
        nc.scalar.activation(out=total[:], in_=total[:], func=ACT.Sqrt, bias=SQRT_GUARD, scale=1.0)
        scores = keep.tile([P, L], F32)
        nc.vector.tensor_scalar_mul(out=scores[:], in0=total[:], scalar1=-1.0)
        nc.sync.dma_start(out=out, in_=scores[:])
